import numpy as np
import ml_dtypes


def mxq(x, axis, fmt="e4m3"):
    dtype, down = {"e4m3": (ml_dtypes.float8_e4m3fn, 7), "e5m2": (ml_dtypes.float8_e5m2, 14)}[fmt]
    v = np.moveaxis(np.asarray(x, np.float32).astype(ml_dtypes.bfloat16).astype(np.float64), axis, -1)
    blocks = v.reshape(v.shape[:-1] + (-1, 32))
    amax = np.abs(blocks).max(-1, keepdims=True)
    byte = np.maximum(np.where(amax > 0, np.frexp(amax)[1] - 1 + 127, 0) - down, 1)
    scale = np.exp2(byte - 127.0)
    codes = (blocks / scale).astype(np.float32).astype(dtype).astype(np.float64)
    return np.moveaxis((codes * scale).reshape(v.shape), -1, axis)


WIDE = False


def mx_kscale(k):
    if not WIDE:
        return np.ones(k)
    levels = np.array([10, -10, 5, -5, 0])
    if k % 512:
        return np.exp2(np.random.permutation(np.resize(levels, k // 32))).repeat(32)
    a = np.empty((k // 512, 16))
    for p in range(k // 512):
        a[p, :8] = np.random.permutation(np.resize(levels, 8))
        for g in range(8):
            far = levels[np.abs(levels - a[p, g]) >= 10]
            a[p, g + 8] = far[np.random.randint(len(far))]
    return np.exp2(a.ravel()).repeat(32)


BF16 = ml_dtypes.bfloat16


def bf(x):
    return np.asarray(x, np.float32).astype(BF16)


def f64(x):
    return np.asarray(x).astype(np.float64)


N, C, H, W, HIDDEN, OUT = 8, 512, 8, 8, 8192, 768
P = H * W
M = N * P


def leaky_relu(v):
    return np.where(v >= 0.0, v, 0.01 * v)


def setup_inputs():
    s, t = mx_kscale(M), mx_kscale(HIDDEN)
    strong = np.where(np.random.random((M, M)) * N < 1.0, 1.0, 0.02)
    weight = np.random.random((M, M)) * strong * 2.0 / P
    hid = leaky_relu(np.random.standard_normal((M, HIDDEN)) * 0.8 - 0.4)
    return {"weight": bf(weight * s[None, :]),
            "hid": bf(hid * t[None, :] / s[:, None]),
            "W2": bf(np.random.standard_normal((OUT, HIDDEN)) * 3.0 / np.sqrt(HIDDEN) / t[None, :]),
            "b2": bf(np.random.standard_normal(OUT) * 0.2 - 0.3)}


def reference(weight, hid, W2, b2):
    agg = mxq(f64(weight), 1, "e4m3") @ mxq(f64(hid), 0, "e4m3")
    y = leaky_relu((mxq(agg, 1, "e4m3") @ mxq(f64(W2), 1, "e4m3").T) + f64(b2))
    y = y.reshape(N, H, W, -1).transpose(0, 3, 1, 2)
    return y.max(axis=0, keepdims=True)

@@ -1,0 +1,262 @@
+import concourse.mybir as mybir
+from concourse.masks import make_identity
+
+F32 = mybir.dt.float32
+BF16 = mybir.dt.bfloat16
+U32 = mybir.dt.uint32
+U8 = mybir.dt.uint8
+FP8X4 = mybir.dt.float8_e4m3fn_x4
+ALU = mybir.AluOpType
+
+P = 128
+PACK = 4
+K_PASS = P * PACK
+HALF = K_PASS // 2
+
+NODES = 512
+HIDDEN = 8192
+OUT = 768
+PIXELS = 64
+SLOPE = 0.01
+
+NODE_TILES = NODES // P
+OUT_TILES = OUT // P
+PASSES = HIDDEN // K_PASS
+CHUNK_PASSES = 2
+CHUNK = CHUNK_PASSES * K_PASS
+CHUNKS = PASSES // CHUNK_PASSES
+GROUPS = ((0, 4), (4, 2))
+STEP_PAIRS = 8
+LOADS_AHEAD = 3
+
+FLOPS = 2 * NODES * NODES * HIDDEN + 2 * NODES * HIDDEN * OUT
+
+
+def flip_two_row_tiles(nc, banks, identity, words, tile0, word0, grouped_words):
+    bank = banks.tile([P, PACK, P], F32, tag="bank")
+    for a in range(2):
+        for u in range(2):
+            nc.tensor.transpose(
+                bank[:, 2 * a + u, :],
+                words[:, tile0 + a, word0 + u : word0 + 2 * P : 2],
+                identity[:],
+            )
+    nc.scalar.copy(
+        out=grouped_words[:, tile0 * P : (tile0 + 2) * P, :].rearrange("p (a r) u -> p a r u", a=2),
+        in_=bank[:].rearrange("p (a u) r -> p a r u", a=2),
+    )
+
+
+def tile_similargcn_pb_k_kernel(tc, weight, hid, W2, b2, out):
+    nc = tc.nc
+    with (
+        tc.tile_pool(name="const", bufs=1) as const,
+        tc.tile_pool(name="keep", bufs=1) as keep,
+        tc.tile_pool(name="raw", bufs=4) as raw,
+        tc.tile_pool(name="stage", bufs=2) as stage,
+        tc.tile_pool(name="codes", bufs=3) as codes,
+        tc.psum_pool(name="sums", bufs=1) as sums,
+        tc.psum_pool(name="banks", bufs=4) as banks,
+        tc.manual_schedule(),
+    ):
+        steps = []
+        for first_tile, n_tiles in GROUPS:
+            step_passes = STEP_PAIRS // n_tiles
+            for first_pass in range(0, PASSES, step_passes):
+                steps.append((first_tile, n_tiles, first_pass, step_passes))
+
+        hid_raw_of = {}
+        hid_grouped_of = {}
+        hid_codes_of = {}
+        w2_raw_of = {}
+        w2_grouped_of = {}
+        w2_codes_of = {}
+        acc_of = {}
+
+        agg_codes = keep.tile([P, PASSES, NODES], U32, align_bytes=64)
+        agg_scales = keep.tile([P, PASSES, NODES], U8, align_bytes=64)
+        result = keep.tile([P, OUT_TILES, PIXELS], F32)
+        out_rows = out.rearrange("x (a p) h w -> p (x a) (h w)", p=P)
+
+        def load(s):
+            if s < CHUNKS:
+                hid_raw = raw.tile([P, PACK, CHUNK], BF16)
+                nc.sync.dma_start(
+                    out=hid_raw[:],
+                    in_=hid[:, s * CHUNK : (s + 1) * CHUNK].rearrange("(q t) f -> q t f", t=PACK),
+                )
+                hid_raw_of[s] = hid_raw
+            first_tile, n_tiles, first_pass, step_passes = steps[s]
+            w2_raw = raw.tile([P, n_tiles, step_passes * K_PASS], BF16, tag="w2_raw")
+            nc.sync.dma_start(
+                out=w2_raw[:],
+                in_=W2[
+                    first_tile * P : (first_tile + n_tiles) * P,
+                    first_pass * K_PASS : (first_pass + step_passes) * K_PASS,
+                ].rearrange("(a p) f -> p a f", p=P),
+            )
+            w2_raw_of[s] = w2_raw
+
+        def flip_w2(s):
+            first_tile, n_tiles, first_pass, step_passes = steps[s]
+            w2_grouped = stage.tile([P, step_passes, n_tiles * P, 2], F32, tag="w2_grouped", align_bytes=64)
+            for local in range(step_passes):
+                for pair in range(n_tiles // 2):
+                    flip_two_row_tiles(
+                        nc, banks, identity, w2_raw_of[s][:].bitcast(F32), 2 * pair, local * HALF,
+                        w2_grouped[:, local],
+                    )
+            w2_grouped_of[s] = w2_grouped
+
+        def quantise_w2(s):
+            first_tile, n_tiles, first_pass, step_passes = steps[s]
+            w2_codes = codes.tile([P, step_passes, n_tiles * P], U32, tag="w2_codes", align_bytes=64)
+            w2_scales = codes.tile([P, step_passes, n_tiles * P], U8, tag="w2_scales", align_bytes=64)
+            nc.vector.quantize_mx(
+                out=w2_codes[:].rearrange("p l o -> p (l o)").bitcast(FP8X4),
+                scales=w2_scales[:].rearrange("p l o -> p (l o)"),
+                in_=w2_grouped_of[s][:].rearrange("p l o u -> p (l o u)").bitcast(BF16),
+            )
+            w2_codes_of[s] = (w2_codes, w2_scales)
+
+        def regroup_hid(c):
+            hid_grouped = stage.tile([P, CHUNK, PACK], BF16, align_bytes=64)
+            nc.vector.tensor_copy(
+                out=hid_grouped[:].rearrange("p (i c) t -> p c t i", i=PACK),
+                in_=hid_raw_of[c][:].rearrange("p t (c i) -> p c t i", i=PACK),
+            )
+            hid_grouped_of[c] = hid_grouped
+
+        def quantise_hid(c):
+            hid_codes = stage.tile([P, CHUNK], U32, align_bytes=64)
+            hid_scales = stage.tile([P, CHUNK], U8, align_bytes=64)
+            nc.vector.quantize_mx(
+                out=hid_codes[:].bitcast(FP8X4),
+                scales=hid_scales[:],
+                in_=hid_grouped_of[c][:].rearrange("p f t -> p (f t)"),
+            )
+            hid_codes_of[c] = (hid_codes, hid_scales)
+
+        def aggregate(c, local, mt, agg_grouped):
+            hid_codes, hid_scales = hid_codes_of[c]
+            m_cols = slice(mt * P, (mt + 1) * P)
+            bank = banks.tile([P, PACK, P], F32, tag="bank")
+            for t in range(PACK):
+                first = t * (CHUNK // PACK) + local * P
+                f_cols = slice(first, first + P)
+                nc.tensor.matmul_mx(
+                    out=bank[:, t, :],
+                    lhsT=hid_codes[:, f_cols].bitcast(FP8X4),
+                    lhsT_scale=hid_scales[:, f_cols],
+                    rhs=weight_codes[:, m_cols].bitcast(FP8X4),
+                    rhs_scale=weight_scales[:, m_cols],
+                    start=True,
+                    stop=True,
+                )
+            nc.scalar.copy(out=agg_grouped[:, m_cols, :], in_=bank[:].rearrange("p t m -> p m t"))
+
+        def multiply(s, i):
+            first_tile, n_tiles, first_pass, step_passes = steps[s]
+            local = i // n_tiles
+            a = i % n_tiles
+            g = first_pass + local
+            if g == 0:
+                acc_of[first_tile + a] = sums.tile([P, NODES], F32, name="acc%d" % a, tag="acc%d" % a)
+            w2_codes, w2_scales = w2_codes_of[s]
+            o_cols = slice(a * P, (a + 1) * P)
+            nc.tensor.matmul_mx(
+                out=acc_of[first_tile + a][:],
+                lhsT=w2_codes[:, local, o_cols].bitcast(FP8X4),
+                lhsT_scale=w2_scales[:, local, o_cols],
+                rhs=agg_codes[:, g, :].bitcast(FP8X4),
+                rhs_scale=agg_scales[:, g, :],
+                start=(g == 0),
+                stop=(g == PASSES - 1),
+            )
+
+        def finish(first_tile, n_tiles):
+            for o_tile in range(first_tile, first_tile + n_tiles):
+                peak = stage.tile([P, PIXELS], F32)
+                nc.vector.tensor_reduce(
+                    out=peak[:],
+                    in_=acc_of[o_tile][:].rearrange("p (n q) -> p q n", q=PIXELS),
+                    axis=mybir.AxisListType.X,
+                    op=ALU.max,
+                )
+                biased = stage.tile([P, PIXELS], F32)
+                nc.vector.tensor_scalar(
+                    out=biased[:], in0=peak[:], scalar1=bias[:, o_tile : o_tile + 1], scalar2=None, op0=ALU.add
+                )
+                nc.vector.scalar_tensor_tensor(
+                    out=result[:, o_tile, :],
+                    in0=biased[:],
+                    scalar=SLOPE,
+                    in1=biased[:],
+                    op0=ALU.mult,
+                    op1=ALU.max,
+                )
+            done = slice(first_tile, first_tile + n_tiles)
+            nc.sync.dma_start(out=out_rows[:, done, :], in_=result[:, done, :])
+
+        identity = const.tile([P, P], F32)
+        make_identity(nc, identity[:])
+        bias_rows = const.tile([P, P], BF16)
+        nc.vector.memset(bias_rows[:], 0.0)
+        nc.sync.dma_start(out=bias_rows[0:OUT_TILES, :], in_=b2.rearrange("(a p) -> a p", p=P))
+        weight_raw = const.tile([P, NODE_TILES, NODES], BF16)
+        nc.sync.dma_start(out=weight_raw[:], in_=weight.rearrange("(a p) j -> p a j", p=P))
+        for s in range(LOADS_AHEAD):
+            load(s)
+
+        bias_rows_f32 = const.tile([P, P], F32)
+        nc.vector.tensor_copy(out=bias_rows_f32[:], in_=bias_rows[:])
+        bias_bank = banks.tile([P, PACK, P], F32, tag="bank")
+        nc.tensor.transpose(bias_bank[:, 0, :], bias_rows_f32[:], identity[:])
+        bias = const.tile([P, OUT_TILES], F32)
+        nc.vector.tensor_copy(out=bias[:], in_=bias_bank[:, 0, 0:OUT_TILES])
+
+        weight_grouped = const.tile([P, NODES, 2], F32, align_bytes=64)
+        for pair in range(NODE_TILES // 2):
+            flip_two_row_tiles(nc, banks, identity, weight_raw[:].bitcast(F32), 2 * pair, 0, weight_grouped)
+        weight_codes = const.tile([P, NODES], U32, align_bytes=64)
+        weight_scales = const.tile([P, NODES], U8, align_bytes=64)
+        flip_w2(0)
+        regroup_hid(0)
+        nc.vector.quantize_mx(
+            out=weight_codes[:].bitcast(FP8X4),
+            scales=weight_scales[:],
+            in_=weight_grouped[:].rearrange("p m u -> p (m u)").bitcast(BF16),
+        )
+        quantise_hid(0)
+
+        for s in range(len(steps) + 1):
+            if s + LOADS_AHEAD < len(steps):
+                load(s + LOADS_AHEAD)
+            if s + 1 < CHUNKS:
+                regroup_hid(s + 1)
+            if s < len(steps):
+                quantise_w2(s)
+            if s + 1 < CHUNKS:
+                quantise_hid(s + 1)
+            for i in range(STEP_PAIRS):
+                if s < CHUNKS:
+                    local = i // NODE_TILES
+                    mt = i % NODE_TILES
+                    if mt == 0:
+                        agg_grouped = stage.tile([P, NODES, PACK], BF16, bufs=3, align_bytes=64)
+                    aggregate(s, local, mt, agg_grouped)
+                    if mt == NODE_TILES - 1:
+                        g = s * CHUNK_PASSES + local
+                        nc.vector.quantize_mx(
+                            out=agg_codes[:, g, :].bitcast(FP8X4),
+                            scales=agg_scales[:, g, :],
+                            in_=agg_grouped[:].rearrange("p m t -> p (m t)"),
+                        )
+                if s >= 1:
+                    multiply(s - 1, i)
+            if s + 1 < len(steps):
+                flip_w2(s + 1)
+            if s >= 1:
+                first_tile, n_tiles, first_pass, step_passes = steps[s - 1]
+                if first_pass + step_passes == PASSES:
+                    finish(first_tile, n_tiles)

@@ -11,7 +11,7 @@ ALU = mybir.AluOpType
 P = 128
 PACK = 4
 K_PASS = P * PACK
-HALF = K_PASS // 2
+WORDS = K_PASS // 2
 
 NODES = 512
 HIDDEN = 8192
@@ -22,27 +22,28 @@ SLOPE = 0.01
 NODE_TILES = NODES // P
 OUT_TILES = OUT // P
 PASSES = HIDDEN // K_PASS
-CHUNK_PASSES = 2
-CHUNK = CHUNK_PASSES * K_PASS
-CHUNKS = PASSES // CHUNK_PASSES
+ROUND_PASSES = 2
+ROUNDS = PASSES // ROUND_PASSES
 GROUPS = ((0, 4), (4, 2))
 STEP_PAIRS = 8
-LOADS_AHEAD = 3
+HID_AHEAD = 2
+W2_AHEAD = 3
+FIRST_LEAD = 0
 
 FLOPS = 2 * NODES * NODES * HIDDEN + 2 * NODES * HIDDEN * OUT
 
 
-def flip_two_row_tiles(nc, banks, identity, words, tile0, word0, grouped_words):
+def split_pairs(s):
+    return 0
+
+
+def flip_two_row_tiles(nc, banks, identity, word_slice, grouped_words):
     bank = banks.tile([P, PACK, P], F32, tag="bank")
     for a in range(2):
         for u in range(2):
-            nc.tensor.transpose(
-                bank[:, 2 * a + u, :],
-                words[:, tile0 + a, word0 + u : word0 + 2 * P : 2],
-                identity[:],
-            )
+            nc.tensor.transpose(bank[:, 2 * a + u, :], word_slice(a, u), identity[:])
     nc.scalar.copy(
-        out=grouped_words[:, tile0 * P : (tile0 + 2) * P, :].rearrange("p (a r) u -> p a r u", a=2),
+        out=grouped_words.rearrange("p (a r) u -> p a r u", a=2),
         in_=bank[:].rearrange("p (a u) r -> p a r u", a=2),
     )
 
@@ -65,10 +66,17 @@ def tile_similargcn_pb_k_kernel(tc, weight, hid, W2, b2, out):
             for first_pass in range(0, PASSES, step_passes):
                 steps.append((first_tile, n_tiles, first_pass, step_passes))
 
+        hid_units = [(0, 1), (1, 1)] + [(g, ROUND_PASSES) for g in range(ROUND_PASSES, PASSES, ROUND_PASSES)]
+        unit_of_pass = {}
+        for c, (first_pass, n_passes) in enumerate(hid_units):
+            for local in range(n_passes):
+                unit_of_pass[first_pass + local] = (c, local)
+
         hid_raw_of = {}
         hid_grouped_of = {}
         hid_codes_of = {}
         w2_raw_of = {}
+        w2_split_of = {}
         w2_grouped_of = {}
         w2_codes_of = {}
         acc_of = {}
@@ -78,49 +86,85 @@ def tile_similargcn_pb_k_kernel(tc, weight, hid, W2, b2, out):
         result = keep.tile([P, OUT_TILES, PIXELS], F32)
         out_rows = out.rearrange("x (a p) h w -> p (x a) (h w)", p=P)
 
-        def load(s):
-            if s < CHUNKS:
-                hid_raw = raw.tile([P, PACK, CHUNK], BF16)
-                nc.sync.dma_start(
-                    out=hid_raw[:],
-                    in_=hid[:, s * CHUNK : (s + 1) * CHUNK].rearrange("(q t) f -> q t f", t=PACK),
-                )
-                hid_raw_of[s] = hid_raw
-            first_tile, n_tiles, first_pass, step_passes = steps[s]
-            w2_raw = raw.tile([P, n_tiles, step_passes * K_PASS], BF16, tag="w2_raw")
+        def load_hid(c):
+            first_pass, n_passes = hid_units[c]
+            hid_raw = raw.tile([P, PACK, n_passes * K_PASS], BF16, tag="hid_raw")
             nc.sync.dma_start(
-                out=w2_raw[:],
-                in_=W2[
-                    first_tile * P : (first_tile + n_tiles) * P,
-                    first_pass * K_PASS : (first_pass + step_passes) * K_PASS,
-                ].rearrange("(a p) f -> p a f", p=P),
+                out=hid_raw[:],
+                in_=hid[:, first_pass * K_PASS : (first_pass + n_passes) * K_PASS].rearrange(
+                    "(q t) f -> q t f", t=PACK
+                ),
             )
+            hid_raw_of[c] = hid_raw
+
+        def load_w2(s, n_loads):
+            first_tile, n_tiles, first_pass, step_passes = steps[s]
+            w2_raw = raw.tile([P, n_tiles, step_passes * K_PASS], BF16, tag="w2_raw", bufs=5)
+            per_load = n_tiles // n_loads
+            for first in range(0, n_tiles, per_load):
+                nc.sync.dma_start(
+                    out=w2_raw[:, first : first + per_load, :],
+                    in_=W2[
+                        (first_tile + first) * P : (first_tile + first + per_load) * P,
+                        first_pass * K_PASS : (first_pass + step_passes) * K_PASS,
+                    ].rearrange("(a p) f -> p a f", p=P),
+                )
             w2_raw_of[s] = w2_raw
+
+        def split_w2(s):
+            first_tile, n_tiles, first_pass, step_passes = steps[s]
+            n_split = 2 * split_pairs(s)
+            if n_split > 0:
+                w2_split = stage.tile([P, n_split, step_passes, 2, P], F32, tag="w2_split", align_bytes=64)
+                nc.vector.tensor_copy(
+                    out=w2_split[:].rearrange("p a l u q -> p (a l) u q"),
+                    in_=w2_raw_of[s][:, 0:n_split, :].bitcast(F32).rearrange("p a (l q u) -> p (a l) u q", q=P, u=2),
+                )
+                w2_split_of[s] = w2_split
 
         def flip_w2(s):
             first_tile, n_tiles, first_pass, step_passes = steps[s]
             w2_grouped = stage.tile([P, step_passes, n_tiles * P, 2], F32, tag="w2_grouped", align_bytes=64)
-            for local in range(step_passes):
-                for pair in range(n_tiles // 2):
-                    flip_two_row_tiles(
-                        nc, banks, identity, w2_raw_of[s][:].bitcast(F32), 2 * pair, local * HALF,
-                        w2_grouped[:, local],
-                    )
             w2_grouped_of[s] = w2_grouped
+            raw_words = w2_raw_of[s][:].bitcast(F32)
+
+            def flip_pair(local, pair):
+                def word_slice(a, u):
+                    if pair < split_pairs(s):
+                        return w2_split_of[s][:, 2 * pair + a, local, u, :]
+                    first = local * WORDS + u
+                    return raw_words[:, 2 * pair + a, first : first + WORDS - u : 2]
+
+                flip_two_row_tiles(
+                    nc, banks, identity, word_slice, w2_grouped[:, local, 2 * pair * P : (2 * pair + 2) * P, :]
+                )
+
+            if s == 0:
+                for pair in range(n_tiles // 2):
+                    for local in range(step_passes):
+                        flip_pair(local, pair)
+            else:
+                for local in range(step_passes):
+                    for pair in range(n_tiles // 2):
+                        flip_pair(local, pair)
 
         def quantise_w2(s):
             first_tile, n_tiles, first_pass, step_passes = steps[s]
             w2_codes = codes.tile([P, step_passes, n_tiles * P], U32, tag="w2_codes", align_bytes=64)
             w2_scales = codes.tile([P, step_passes, n_tiles * P], U8, tag="w2_scales", align_bytes=64)
-            nc.vector.quantize_mx(
-                out=w2_codes[:].rearrange("p l o -> p (l o)").bitcast(FP8X4),
-                scales=w2_scales[:].rearrange("p l o -> p (l o)"),
-                in_=w2_grouped_of[s][:].rearrange("p l o u -> p (l o u)").bitcast(BF16),
-            )
+            per_call = 2 if s >= ROUNDS else step_passes
+            for first in range(0, step_passes, per_call):
+                part = slice(first, first + per_call)
+                nc.vector.quantize_mx(
+                    out=w2_codes[:, part, :].rearrange("p l o -> p (l o)").bitcast(FP8X4),
+                    scales=w2_scales[:, part, :].rearrange("p l o -> p (l o)"),
+                    in_=w2_grouped_of[s][:, part, :, :].rearrange("p l o u -> p (l o u)").bitcast(BF16),
+                )
             w2_codes_of[s] = (w2_codes, w2_scales)
 
         def regroup_hid(c):
-            hid_grouped = stage.tile([P, CHUNK, PACK], BF16, align_bytes=64)
+            width = hid_units[c][1] * K_PASS
+            hid_grouped = stage.tile([P, width, PACK], BF16, tag="hid_grouped", align_bytes=64)
             nc.vector.tensor_copy(
                 out=hid_grouped[:].rearrange("p (i c) t -> p c t i", i=PACK),
                 in_=hid_raw_of[c][:].rearrange("p t (c i) -> p c t i", i=PACK),
@@ -128,8 +172,9 @@ def tile_similargcn_pb_k_kernel(tc, weight, hid, W2, b2, out):
             hid_grouped_of[c] = hid_grouped
 
         def quantise_hid(c):
-            hid_codes = stage.tile([P, CHUNK], U32, align_bytes=64)
-            hid_scales = stage.tile([P, CHUNK], U8, align_bytes=64)
+            width = hid_units[c][1] * K_PASS
+            hid_codes = stage.tile([P, width], U32, tag="hid_codes", bufs=3, align_bytes=64)
+            hid_scales = stage.tile([P, width], U8, tag="hid_scales", bufs=3, align_bytes=64)
             nc.vector.quantize_mx(
                 out=hid_codes[:].bitcast(FP8X4),
                 scales=hid_scales[:],
@@ -137,12 +182,18 @@ def tile_similargcn_pb_k_kernel(tc, weight, hid, W2, b2, out):
             )
             hid_codes_of[c] = (hid_codes, hid_scales)
 
-        def aggregate(c, local, mt, agg_grouped):
+        agg_grouped_of = {}
+
+        def aggregate(g, mt):
+            if mt == 0:
+                agg_grouped = stage.tile([P, NODES, PACK], BF16, bufs=3, align_bytes=64)
+                agg_grouped_of[g] = agg_grouped
+            c, local = unit_of_pass[g]
             hid_codes, hid_scales = hid_codes_of[c]
             m_cols = slice(mt * P, (mt + 1) * P)
             bank = banks.tile([P, PACK, P], F32, tag="bank")
             for t in range(PACK):
-                first = t * (CHUNK // PACK) + local * P
+                first = (t * hid_units[c][1] + local) * P
                 f_cols = slice(first, first + P)
                 nc.tensor.matmul_mx(
                     out=bank[:, t, :],
@@ -153,12 +204,20 @@ def tile_similargcn_pb_k_kernel(tc, weight, hid, W2, b2, out):
                     start=True,
                     stop=True,
                 )
-            nc.scalar.copy(out=agg_grouped[:, m_cols, :], in_=bank[:].rearrange("p t m -> p m t"))
+            nc.scalar.copy(out=agg_grouped_of[g][:, m_cols, :], in_=bank[:].rearrange("p t m -> p m t"))
+
+        def quantise_agg(g):
+            nc.vector.quantize_mx(
+                out=agg_codes[:, g, :].bitcast(FP8X4),
+                scales=agg_scales[:, g, :],
+                in_=agg_grouped_of[g][:].rearrange("p m t -> p (m t)"),
+            )
 
         def multiply(s, i):
             first_tile, n_tiles, first_pass, step_passes = steps[s]
-            local = i // n_tiles
-            a = i % n_tiles
+            by_tile = s in (ROUNDS - 1, ROUNDS, len(steps) - 1)
+            local = i % step_passes if by_tile else i // n_tiles
+            a = i // step_passes if by_tile else i % n_tiles
             g = first_pass + local
             if g == 0:
                 acc_of[first_tile + a] = sums.tile([P, NODES], F32, name="acc%d" % a, tag="acc%d" % a)
@@ -173,90 +232,120 @@ def tile_similargcn_pb_k_kernel(tc, weight, hid, W2, b2, out):
                 start=(g == 0),
                 stop=(g == PASSES - 1),
             )
+            if g == PASSES - 1:
+                finish(first_tile + a)
 
-        def finish(first_tile, n_tiles):
-            for o_tile in range(first_tile, first_tile + n_tiles):
-                peak = stage.tile([P, PIXELS], F32)
-                nc.vector.tensor_reduce(
-                    out=peak[:],
-                    in_=acc_of[o_tile][:].rearrange("p (n q) -> p q n", q=PIXELS),
-                    axis=mybir.AxisListType.X,
-                    op=ALU.max,
-                )
-                biased = stage.tile([P, PIXELS], F32)
-                nc.vector.tensor_scalar(
-                    out=biased[:], in0=peak[:], scalar1=bias[:, o_tile : o_tile + 1], scalar2=None, op0=ALU.add
-                )
-                nc.vector.scalar_tensor_tensor(
-                    out=result[:, o_tile, :],
-                    in0=biased[:],
-                    scalar=SLOPE,
-                    in1=biased[:],
-                    op0=ALU.mult,
-                    op1=ALU.max,
-                )
-            done = slice(first_tile, first_tile + n_tiles)
-            nc.sync.dma_start(out=out_rows[:, done, :], in_=result[:, done, :])
+        def finish(o_tile):
+            peak = stage.tile([P, PIXELS], F32)
+            nc.vector.tensor_reduce(
+                out=peak[:],
+                in_=acc_of[o_tile][:].rearrange("p (n q) -> p q n", q=PIXELS),
+                axis=mybir.AxisListType.X,
+                op=ALU.max,
+            )
+            biased = stage.tile([P, PIXELS], F32)
+            nc.vector.tensor_scalar(
+                out=biased[:], in0=peak[:], scalar1=bias[:, o_tile : o_tile + 1], scalar2=None, op0=ALU.add
+            )
+            nc.vector.scalar_tensor_tensor(
+                out=result[:, o_tile, :],
+                in0=biased[:],
+                scalar=SLOPE,
+                in1=biased[:],
+                op0=ALU.mult,
+                op1=ALU.max,
+            )
+            if o_tile >= NODE_TILES - 1:
+                first = 0 if o_tile == NODE_TILES - 1 else o_tile
+                nc.sync.dma_start(out=out_rows[:, first : o_tile + 1, :], in_=result[:, first : o_tile + 1, :])
 
         identity = const.tile([P, P], F32)
         make_identity(nc, identity[:])
         bias_rows = const.tile([P, P], BF16)
         nc.vector.memset(bias_rows[:], 0.0)
-        nc.sync.dma_start(out=bias_rows[0:OUT_TILES, :], in_=b2.rearrange("(a p) -> a p", p=P))
+        load_hid(0)
         weight_raw = const.tile([P, NODE_TILES, NODES], BF16)
-        nc.sync.dma_start(out=weight_raw[:], in_=weight.rearrange("(a p) j -> p a j", p=P))
-        for s in range(LOADS_AHEAD):
-            load(s)
+        for pair in range(NODE_TILES // 2):
+            nc.sync.dma_start(
+                out=weight_raw[:, 2 * pair : 2 * pair + 2, :],
+                in_=weight[2 * pair * P : (2 * pair + 2) * P, :].rearrange("(a p) j -> p a j", p=P),
+            )
+        load_hid(1)
+        load_w2(0, 2)
+        nc.sync.dma_start(out=bias_rows[0:OUT_TILES, :], in_=b2.rearrange("(a p) -> a p", p=P))
+        load_hid(2)
+        load_w2(1, 1)
+        load_w2(2, 1)
+        load_hid(3)
+        load_w2(3, 1)
 
+        regroup_hid(0)
+        weight_grouped = const.tile([P, NODES, 2], F32, align_bytes=64)
+        weight_codes = const.tile([P, NODES], U32, align_bytes=64)
+        weight_scales = const.tile([P, NODES], U8, align_bytes=64)
+        for pair in range(NODE_TILES // 2):
+            pair_words = weight_raw[:, 2 * pair : 2 * pair + 2, :].bitcast(F32)
+            flip_two_row_tiles(
+                nc,
+                banks,
+                identity,
+                lambda a, u, words=pair_words: words[:, a, u : WORDS : 2],
+                weight_grouped[:, 2 * pair * P : (2 * pair + 2) * P, :],
+            )
+        quantise_hid(0)
+        for pair in range(NODE_TILES // 2):
+            m_cols = slice(2 * pair * P, (2 * pair + 2) * P)
+            nc.vector.quantize_mx(
+                out=weight_codes[:, m_cols].bitcast(FP8X4),
+                scales=weight_scales[:, m_cols],
+                in_=weight_grouped[:, m_cols, :].rearrange("p m u -> p (m u)").bitcast(BF16),
+            )
+        regroup_hid(1)
+        for mt in range(NODE_TILES):
+            aggregate(0, mt)
+        flip_w2(0)
+        quantise_hid(1)
+        quantise_agg(0)
+        for mt in range(NODE_TILES):
+            aggregate(1, mt)
         bias_rows_f32 = const.tile([P, P], F32)
         nc.vector.tensor_copy(out=bias_rows_f32[:], in_=bias_rows[:])
+        regroup_hid(2)
+        quantise_w2(0)
+        quantise_agg(1)
+        quantise_hid(2)
+        flip_w2(1)
         bias_bank = banks.tile([P, PACK, P], F32, tag="bank")
         nc.tensor.transpose(bias_bank[:, 0, :], bias_rows_f32[:], identity[:])
         bias = const.tile([P, OUT_TILES], F32)
-        nc.vector.tensor_copy(out=bias[:], in_=bias_bank[:, 0, 0:OUT_TILES])
+        nc.scalar.copy(out=bias[:], in_=bias_bank[:, 0, 0:OUT_TILES])
+        split_w2(2)
 
-        weight_grouped = const.tile([P, NODES, 2], F32, align_bytes=64)
-        for pair in range(NODE_TILES // 2):
-            flip_two_row_tiles(nc, banks, identity, weight_raw[:].bitcast(F32), 2 * pair, 0, weight_grouped)
-        weight_codes = const.tile([P, NODES], U32, align_bytes=64)
-        weight_scales = const.tile([P, NODES], U8, align_bytes=64)
-        flip_w2(0)
-        regroup_hid(0)
-        nc.vector.quantize_mx(
-            out=weight_codes[:].bitcast(FP8X4),
-            scales=weight_scales[:],
-            in_=weight_grouped[:].rearrange("p m u -> p (m u)").bitcast(BF16),
-        )
-        quantise_hid(0)
-
-        for s in range(len(steps) + 1):
-            if s + LOADS_AHEAD < len(steps):
-                load(s + LOADS_AHEAD)
-            if s + 1 < CHUNKS:
-                regroup_hid(s + 1)
+        for s in range(1, len(steps) + 1):
+            if s + HID_AHEAD < ROUNDS:
+                load_hid(s + HID_AHEAD + 1)
+            if s + W2_AHEAD < len(steps):
+                load_w2(s + W2_AHEAD, 1)
+            if s + 1 < ROUNDS:
+                regroup_hid(s + 2)
             if s < len(steps):
                 quantise_w2(s)
-            if s + 1 < CHUNKS:
-                quantise_hid(s + 1)
+            if s + 1 < ROUNDS:
+                quantise_hid(s + 2)
+            if s >= ROUNDS and s + 2 < len(steps):
+                split_w2(s + 2)
+            lead = FIRST_LEAD if s == 1 else 0
+            for i in range(lead):
+                multiply(s - 1, i)
             for i in range(STEP_PAIRS):
-                if s < CHUNKS:
-                    local = i // NODE_TILES
-                    mt = i % NODE_TILES
-                    if mt == 0:
-                        agg_grouped = stage.tile([P, NODES, PACK], BF16, bufs=3, align_bytes=64)
-                    aggregate(s, local, mt, agg_grouped)
-                    if mt == NODE_TILES - 1:
-                        g = s * CHUNK_PASSES + local
-                        nc.vector.quantize_mx(
-                            out=agg_codes[:, g, :].bitcast(FP8X4),
-                            scales=agg_scales[:, g, :],
-                            in_=agg_grouped[:].rearrange("p m t -> p (m t)"),
-                        )
-                if s >= 1:
-                    multiply(s - 1, i)
+                if s < ROUNDS:
+                    g = s * ROUND_PASSES + i // NODE_TILES
+                    aggregate(g, i % NODE_TILES)
+                    if i % NODE_TILES == NODE_TILES - 1:
+                        quantise_agg(g)
+                if i + lead < STEP_PAIRS:
+                    multiply(s - 1, i + lead)
+            if s < ROUNDS and s + 2 < len(steps):
+                split_w2(s + 2)
             if s + 1 < len(steps):
                 flip_w2(s + 1)
-            if s >= 1:
-                first_tile, n_tiles, first_pass, step_passes = steps[s - 1]
-                if first_pass + step_passes == PASSES:
-                    finish(first_tile, n_tiles)

@@ -34,7 +34,7 @@ FLOPS = 2 * NODES * NODES * HIDDEN + 2 * NODES * HIDDEN * OUT
 
 
 def split_pairs(s):
-    return 0
+    return 0 if s < 2 else 1
 
 
 def flip_two_row_tiles(nc, banks, identity, word_slice, grouped_words):

@@ -27,14 +27,14 @@ ROUNDS = PASSES // ROUND_PASSES
 GROUPS = ((0, 4), (4, 2))
 STEP_PAIRS = 8
 HID_AHEAD = 2
+FIRST_SINGLES = 4
 W2_AHEAD = 3
-FIRST_LEAD = 0
 
 FLOPS = 2 * NODES * NODES * HIDDEN + 2 * NODES * HIDDEN * OUT
 
 
 def split_pairs(s):
-    return 0 if s < 2 else 1
+    return 0 if s < 3 else 1
 
 
 def flip_two_row_tiles(nc, banks, identity, word_slice, grouped_words):
@@ -66,7 +66,9 @@ def tile_similargcn_pb_k_kernel(tc, weight, hid, W2, b2, out):
             for first_pass in range(0, PASSES, step_passes):
                 steps.append((first_tile, n_tiles, first_pass, step_passes))
 
-        hid_units = [(0, 1), (1, 1)] + [(g, ROUND_PASSES) for g in range(ROUND_PASSES, PASSES, ROUND_PASSES)]
+        hid_units = [(g, 1) for g in range(FIRST_SINGLES)] + [
+            (g, ROUND_PASSES) for g in range(FIRST_SINGLES, PASSES, ROUND_PASSES)
+        ]
         unit_of_pass = {}
         for c, (first_pass, n_passes) in enumerate(hid_units):
             for local in range(n_passes):
@@ -83,6 +85,8 @@ def tile_similargcn_pb_k_kernel(tc, weight, hid, W2, b2, out):
 
         agg_codes = keep.tile([P, PASSES, NODES], U32, align_bytes=64)
         agg_scales = keep.tile([P, PASSES, NODES], U8, align_bytes=64)
+        peaks = keep.tile([P, OUT_TILES, PIXELS], F32)
+        biased = keep.tile([P, OUT_TILES, PIXELS], F32)
         result = keep.tile([P, OUT_TILES, PIXELS], F32)
         out_rows = out.rearrange("x (a p) h w -> p (x a) (h w)", p=P)
 
@@ -136,7 +140,11 @@ def tile_similargcn_pb_k_kernel(tc, weight, hid, W2, b2, out):
                     return raw_words[:, 2 * pair + a, first : first + WORDS - u : 2]
 
                 flip_two_row_tiles(
-                    nc, banks, identity, word_slice, w2_grouped[:, local, 2 * pair * P : (2 * pair + 2) * P, :]
+                    nc,
+                    banks,
+                    identity,
+                    word_slice,
+                    w2_grouped[:, local, 2 * pair * P : (2 * pair + 2) * P, :],
                 )
 
             if s == 0:
@@ -233,31 +241,37 @@ def tile_similargcn_pb_k_kernel(tc, weight, hid, W2, b2, out):
                 stop=(g == PASSES - 1),
             )
             if g == PASSES - 1:
-                finish(first_tile + a)
+                take_peak(first_tile + a)
+                if first_tile > 0:
+                    finish(first_tile + a, 1)
 
-        def finish(o_tile):
-            peak = stage.tile([P, PIXELS], F32)
+        def take_peak(o_tile):
             nc.vector.tensor_reduce(
-                out=peak[:],
+                out=peaks[:, o_tile, :],
                 in_=acc_of[o_tile][:].rearrange("p (n q) -> p q n", q=PIXELS),
                 axis=mybir.AxisListType.X,
                 op=ALU.max,
             )
-            biased = stage.tile([P, PIXELS], F32)
-            nc.vector.tensor_scalar(
-                out=biased[:], in0=peak[:], scalar1=bias[:, o_tile : o_tile + 1], scalar2=None, op0=ALU.add
-            )
+
+        def finish(first_tile, n_tiles):
+            done = slice(first_tile, first_tile + n_tiles)
+            for o_tile in range(first_tile, first_tile + n_tiles):
+                nc.vector.tensor_scalar(
+                    out=biased[:, o_tile, :],
+                    in0=peaks[:, o_tile, :],
+                    scalar1=bias[:, o_tile : o_tile + 1],
+                    scalar2=None,
+                    op0=ALU.add,
+                )
             nc.vector.scalar_tensor_tensor(
-                out=result[:, o_tile, :],
-                in0=biased[:],
+                out=result[:, done, :],
+                in0=biased[:, done, :],
                 scalar=SLOPE,
-                in1=biased[:],
+                in1=biased[:, done, :],
                 op0=ALU.mult,
                 op1=ALU.max,
             )
-            if o_tile >= NODE_TILES - 1:
-                first = 0 if o_tile == NODE_TILES - 1 else o_tile
-                nc.sync.dma_start(out=out_rows[:, first : o_tile + 1, :], in_=result[:, first : o_tile + 1, :])
+            nc.sync.dma_start(out=out_rows[:, done, :], in_=result[:, done, :])
 
         identity = const.tile([P, P], F32)
         make_identity(nc, identity[:])
@@ -275,15 +289,15 @@ def tile_similargcn_pb_k_kernel(tc, weight, hid, W2, b2, out):
         nc.sync.dma_start(out=bias_rows[0:OUT_TILES, :], in_=b2.rearrange("(a p) -> a p", p=P))
         load_hid(2)
         load_w2(1, 1)
-        load_w2(2, 1)
         load_hid(3)
+        load_w2(2, 1)
+        load_hid(4)
         load_w2(3, 1)
-
-        regroup_hid(0)
         weight_grouped = const.tile([P, NODES, 2], F32, align_bytes=64)
         weight_codes = const.tile([P, NODES], U32, align_bytes=64)
         weight_scales = const.tile([P, NODES], U8, align_bytes=64)
-        for pair in range(NODE_TILES // 2):
+
+        def flip_weight(pair):
             pair_words = weight_raw[:, 2 * pair : 2 * pair + 2, :].bitcast(F32)
             flip_two_row_tiles(
                 nc,
@@ -292,60 +306,78 @@ def tile_similargcn_pb_k_kernel(tc, weight, hid, W2, b2, out):
                 lambda a, u, words=pair_words: words[:, a, u : WORDS : 2],
                 weight_grouped[:, 2 * pair * P : (2 * pair + 2) * P, :],
             )
-        quantise_hid(0)
-        for pair in range(NODE_TILES // 2):
+
+        def quantise_weight(pair):
             m_cols = slice(2 * pair * P, (2 * pair + 2) * P)
             nc.vector.quantize_mx(
                 out=weight_codes[:, m_cols].bitcast(FP8X4),
                 scales=weight_scales[:, m_cols],
                 in_=weight_grouped[:, m_cols, :].rearrange("p m u -> p (m u)").bitcast(BF16),
             )
+
+        def aggregate_pass(g):
+            for mt in range(NODE_TILES):
+                aggregate(g, mt)
+
+        bias_rows_f32 = const.tile([P, P], F32)
+        bias = const.tile([P, OUT_TILES], F32)
+
+        def spread_bias():
+            nc.vector.tensor_copy(out=bias_rows_f32[:], in_=bias_rows[:])
+
+        def flip_bias():
+            bias_bank = banks.tile([P, PACK, P], F32, tag="bank")
+            nc.tensor.transpose(bias_bank[:, 0, :], bias_rows_f32[:], identity[:])
+            nc.scalar.copy(out=bias[:], in_=bias_bank[:, 0, 0:OUT_TILES])
+
+        regroup_hid(0)
+        flip_weight(0)
+        flip_weight(1)
+        quantise_hid(0)
+        quantise_weight(0)
+        quantise_weight(1)
         regroup_hid(1)
-        for mt in range(NODE_TILES):
-            aggregate(0, mt)
+        aggregate_pass(0)
         flip_w2(0)
         quantise_hid(1)
         quantise_agg(0)
-        for mt in range(NODE_TILES):
-            aggregate(1, mt)
-        bias_rows_f32 = const.tile([P, P], F32)
-        nc.vector.tensor_copy(out=bias_rows_f32[:], in_=bias_rows[:])
+        aggregate_pass(1)
+        spread_bias()
         regroup_hid(2)
         quantise_w2(0)
-        quantise_agg(1)
         quantise_hid(2)
+        regroup_hid(3)
+        quantise_agg(1)
+        quantise_hid(3)
         flip_w2(1)
-        bias_bank = banks.tile([P, PACK, P], F32, tag="bank")
-        nc.tensor.transpose(bias_bank[:, 0, :], bias_rows_f32[:], identity[:])
-        bias = const.tile([P, OUT_TILES], F32)
-        nc.scalar.copy(out=bias[:], in_=bias_bank[:, 0, 0:OUT_TILES])
+        flip_bias()
         split_w2(2)
 
         for s in range(1, len(steps) + 1):
             if s + HID_AHEAD < ROUNDS:
-                load_hid(s + HID_AHEAD + 1)
+                load_hid(s + HID_AHEAD + 3 - 1)
             if s + W2_AHEAD < len(steps):
                 load_w2(s + W2_AHEAD, 1)
+            if s > 1 and s <= ROUNDS:
+                quantise_agg(s * ROUND_PASSES - 1)
             if s + 1 < ROUNDS:
-                regroup_hid(s + 2)
+                regroup_hid(s + 3)
             if s < len(steps):
                 quantise_w2(s)
             if s + 1 < ROUNDS:
-                quantise_hid(s + 2)
-            if s >= ROUNDS and s + 2 < len(steps):
+                quantise_hid(s + 3)
+            if s >= (ROUNDS + 1) and s + 2 < len(steps):
                 split_w2(s + 2)
-            lead = FIRST_LEAD if s == 1 else 0
-            for i in range(lead):
-                multiply(s - 1, i)
             for i in range(STEP_PAIRS):
                 if s < ROUNDS:
                     g = s * ROUND_PASSES + i // NODE_TILES
                     aggregate(g, i % NODE_TILES)
-                    if i % NODE_TILES == NODE_TILES - 1:
+                    if i % NODE_TILES == NODE_TILES - 1 and i < STEP_PAIRS - 1:
                         quantise_agg(g)
-                if i + lead < STEP_PAIRS:
-                    multiply(s - 1, i + lead)
-            if s < ROUNDS and s + 2 < len(steps):
+                multiply(s - 1, i)
+            if s < (ROUNDS + 1) and s + 2 < len(steps):
                 split_w2(s + 2)
             if s + 1 < len(steps):
                 flip_w2(s + 1)
+            if s == ROUNDS + 1:
+                finish(0, NODE_TILES)

@@ -34,7 +34,7 @@ FLOPS = 2 * NODES * NODES * HIDDEN + 2 * NODES * HIDDEN * OUT
 
 
 def split_pairs(s):
-    return 0 if s < 3 else 1
+    return 1 if s >= ROUNDS else 0
 
 
 def flip_two_row_tiles(nc, banks, identity, word_slice, grouped_words):
@@ -290,8 +290,8 @@ def tile_similargcn_pb_k_kernel(tc, weight, hid, W2, b2, out):
         load_hid(2)
         load_w2(1, 1)
         load_hid(3)
-        load_w2(2, 1)
         load_hid(4)
+        load_w2(2, 1)
         load_w2(3, 1)
         weight_grouped = const.tile([P, NODES, 2], F32, align_bytes=64)
         weight_codes = const.tile([P, NODES], U32, align_bytes=64)

@@ -24,26 +24,25 @@ OUT_TILES = OUT // P
 PASSES = HIDDEN // K_PASS
 ROUND_PASSES = 2
 ROUNDS = PASSES // ROUND_PASSES
-GROUPS = ((0, 4), (4, 2))
-STEP_PAIRS = 8
+GROUPS = ((0, 4, 2), (4, 2, 4))
 HID_AHEAD = 2
 FIRST_SINGLES = 4
-W2_AHEAD = 3
+W2_AHEAD = 2
 
 FLOPS = 2 * NODES * NODES * HIDDEN + 2 * NODES * HIDDEN * OUT
 
 
-def split_pairs(s):
-    return 1 if s >= ROUNDS else 0
+def split_tiles(s):
+    return 2 if s >= ROUNDS else (1 if s > 4 else 0)
 
 
-def flip_two_row_tiles(nc, banks, identity, word_slice, grouped_words):
+def flip_pair(nc, banks, identity, word_slice, grouped_words):
     bank = banks.tile([P, PACK, P], F32, tag="bank")
     for a in range(2):
         for u in range(2):
             nc.tensor.transpose(bank[:, 2 * a + u, :], word_slice(a, u), identity[:])
     nc.scalar.copy(
-        out=grouped_words.rearrange("p (a r) u -> p a r u", a=2),
+        out=grouped_words,
         in_=bank[:].rearrange("p (a u) r -> p a r u", a=2),
     )
 
@@ -61,8 +60,7 @@ def tile_similargcn_pb_k_kernel(tc, weight, hid, W2, b2, out):
         tc.manual_schedule(),
     ):
         steps = []
-        for first_tile, n_tiles in GROUPS:
-            step_passes = STEP_PAIRS // n_tiles
+        for first_tile, n_tiles, step_passes in GROUPS:
             for first_pass in range(0, PASSES, step_passes):
                 steps.append((first_tile, n_tiles, first_pass, step_passes))
 
@@ -82,12 +80,15 @@ def tile_similargcn_pb_k_kernel(tc, weight, hid, W2, b2, out):
         w2_grouped_of = {}
         w2_codes_of = {}
         acc_of = {}
+        acc_halves = []
 
         agg_codes = keep.tile([P, PASSES, NODES], U32, align_bytes=64)
         agg_scales = keep.tile([P, PASSES, NODES], U8, align_bytes=64)
         peaks = keep.tile([P, OUT_TILES, PIXELS], F32)
         biased = keep.tile([P, OUT_TILES, PIXELS], F32)
         result = keep.tile([P, OUT_TILES, PIXELS], F32)
+        half_peaks = keep.tile([P, 2, PIXELS], F32)
+        half_biased = keep.tile([P, PIXELS], F32)
         out_rows = out.rearrange("x (a p) h w -> p (x a) (h w)", p=P)
 
         def load_hid(c):
@@ -101,23 +102,28 @@ def tile_similargcn_pb_k_kernel(tc, weight, hid, W2, b2, out):
             )
             hid_raw_of[c] = hid_raw
 
-        def load_w2(s, n_loads):
-            first_tile, n_tiles, first_pass, step_passes = steps[s]
-            w2_raw = raw.tile([P, n_tiles, step_passes * K_PASS], BF16, tag="w2_raw", bufs=5)
+        def load_w2(s, n_loads=1):
+            n_tiles = steps[s][1]
             per_load = n_tiles // n_loads
             for first in range(0, n_tiles, per_load):
-                nc.sync.dma_start(
-                    out=w2_raw[:, first : first + per_load, :],
-                    in_=W2[
-                        (first_tile + first) * P : (first_tile + first + per_load) * P,
-                        first_pass * K_PASS : (first_pass + step_passes) * K_PASS,
-                    ].rearrange("(a p) f -> p a f", p=P),
-                )
-            w2_raw_of[s] = w2_raw
+                load_w2_tiles(s, first, per_load)
+
+        def load_w2_tiles(s, first, per_load):
+            first_tile, n_tiles, first_pass, step_passes = steps[s]
+            if s not in w2_raw_of:
+                w2_raw = raw.tile([P, n_tiles, step_passes * K_PASS], BF16, tag="w2_raw", bufs=5)
+                w2_raw_of[s] = w2_raw
+            nc.sync.dma_start(
+                out=w2_raw_of[s][:, first : first + per_load, :],
+                in_=W2[
+                    (first_tile + first) * P : (first_tile + first + per_load) * P,
+                    first_pass * K_PASS : (first_pass + step_passes) * K_PASS,
+                ].rearrange("(a p) f -> p a f", p=P),
+            )
 
         def split_w2(s):
             first_tile, n_tiles, first_pass, step_passes = steps[s]
-            n_split = 2 * split_pairs(s)
+            n_split = split_tiles(s)
             if n_split > 0:
                 w2_split = stage.tile([P, n_split, step_passes, 2, P], F32, tag="w2_split", align_bytes=64)
                 nc.vector.tensor_copy(
@@ -126,47 +132,43 @@ def tile_similargcn_pb_k_kernel(tc, weight, hid, W2, b2, out):
                 )
                 w2_split_of[s] = w2_split
 
-        def flip_w2(s):
+        def start_flips(s):
             first_tile, n_tiles, first_pass, step_passes = steps[s]
-            w2_grouped = stage.tile([P, step_passes, n_tiles * P, 2], F32, tag="w2_grouped", align_bytes=64)
+            w2_grouped = stage.tile([P, n_tiles, step_passes, P, 2], F32, tag="w2_grouped", align_bytes=64)
             w2_grouped_of[s] = w2_grouped
+
+        def flip_tile(s, a, first_local):
             raw_words = w2_raw_of[s][:].bitcast(F32)
 
-            def flip_pair(local, pair):
-                def word_slice(a, u):
-                    if pair < split_pairs(s):
-                        return w2_split_of[s][:, 2 * pair + a, local, u, :]
-                    first = local * WORDS + u
-                    return raw_words[:, 2 * pair + a, first : first + WORDS - u : 2]
+            def word_slice(j, u):
+                local = first_local + j
+                if a < split_tiles(s):
+                    return w2_split_of[s][:, a, local, u, :]
+                first = local * WORDS + u
+                return raw_words[:, a, first : first + WORDS - u : 2]
 
-                flip_two_row_tiles(
-                    nc,
-                    banks,
-                    identity,
-                    word_slice,
-                    w2_grouped[:, local, 2 * pair * P : (2 * pair + 2) * P, :],
-                )
+            flip_pair(nc, banks, identity, word_slice, w2_grouped_of[s][:, a, first_local : first_local + 2, :, :])
 
-            if s == 0:
-                for pair in range(n_tiles // 2):
-                    for local in range(step_passes):
-                        flip_pair(local, pair)
-            else:
-                for local in range(step_passes):
-                    for pair in range(n_tiles // 2):
-                        flip_pair(local, pair)
+        def flip_w2(s):
+            first_tile, n_tiles, first_pass, step_passes = steps[s]
+            start_flips(s)
+            for a in range(n_tiles):
+                for first_local in range(0, step_passes, 2):
+                    flip_tile(s, a, first_local)
 
         def quantise_w2(s):
             first_tile, n_tiles, first_pass, step_passes = steps[s]
-            w2_codes = codes.tile([P, step_passes, n_tiles * P], U32, tag="w2_codes", align_bytes=64)
-            w2_scales = codes.tile([P, step_passes, n_tiles * P], U8, tag="w2_scales", align_bytes=64)
-            per_call = 2 if s >= ROUNDS else step_passes
-            for first in range(0, step_passes, per_call):
-                part = slice(first, first + per_call)
+            w2_codes = codes.tile([P, n_tiles, step_passes, P], U32, tag="w2_codes", align_bytes=64)
+            w2_scales = codes.tile([P, n_tiles, step_passes, P], U8, tag="w2_scales", align_bytes=64)
+            calls = (n_tiles,) if s < ROUNDS else (1, 1)
+            first = 0
+            for count in calls:
+                part = slice(first, first + count)
+                first = first + count
                 nc.vector.quantize_mx(
-                    out=w2_codes[:, part, :].rearrange("p l o -> p (l o)").bitcast(FP8X4),
-                    scales=w2_scales[:, part, :].rearrange("p l o -> p (l o)"),
-                    in_=w2_grouped_of[s][:, part, :, :].rearrange("p l o u -> p (l o u)").bitcast(BF16),
+                    out=w2_codes[:, part].rearrange("p a l o -> p (a l o)").bitcast(FP8X4),
+                    scales=w2_scales[:, part].rearrange("p a l o -> p (a l o)"),
+                    in_=w2_grouped_of[s][:, part].rearrange("p a l o u -> p (a l o u)").bitcast(BF16),
                 )
             w2_codes_of[s] = (w2_codes, w2_scales)
 
@@ -223,46 +225,90 @@ def tile_similargcn_pb_k_kernel(tc, weight, hid, W2, b2, out):
 
         def multiply(s, i):
             first_tile, n_tiles, first_pass, step_passes = steps[s]
+            last_step = s == len(steps) - 1
             by_tile = s in (ROUNDS - 1, ROUNDS, len(steps) - 1)
             local = i % step_passes if by_tile else i // n_tiles
             a = i // step_passes if by_tile else i % n_tiles
             g = first_pass + local
+            w2_codes, w2_scales = w2_codes_of[s]
+            if first_tile + a == OUT_TILES - 1:
+                if g == 0:
+                    for half in range(2):
+                        acc_half = sums.tile([P, NODES // 2], F32, name="acc_half%d" % half, tag="acc%d" % (a + half))
+                        acc_halves.append(acc_half)
+                for j in range(2):
+                    unit = 2 * local + j
+                    half = unit // step_passes if last_step else j
+                    pass_of_unit = unit % step_passes if last_step else local
+                    multiply_half(s, a, pass_of_unit, half)
+                return
             if g == 0:
                 acc_of[first_tile + a] = sums.tile([P, NODES], F32, name="acc%d" % a, tag="acc%d" % a)
-            w2_codes, w2_scales = w2_codes_of[s]
-            o_cols = slice(a * P, (a + 1) * P)
             nc.tensor.matmul_mx(
                 out=acc_of[first_tile + a][:],
-                lhsT=w2_codes[:, local, o_cols].bitcast(FP8X4),
-                lhsT_scale=w2_scales[:, local, o_cols],
+                lhsT=w2_codes[:, a, local, :].bitcast(FP8X4),
+                lhsT_scale=w2_scales[:, a, local, :],
                 rhs=agg_codes[:, g, :].bitcast(FP8X4),
                 rhs_scale=agg_scales[:, g, :],
                 start=(g == 0),
                 stop=(g == PASSES - 1),
             )
             if g == PASSES - 1:
-                take_peak(first_tile + a)
-                if first_tile > 0:
-                    finish(first_tile + a, 1)
+                take_peak(peaks[:, first_tile + a, :], acc_of[first_tile + a])
 
-        def take_peak(o_tile):
+        def multiply_half(s, a, local, half):
+            g = steps[s][2] + local
+            w2_codes, w2_scales = w2_codes_of[s]
+            n_cols = slice(half * NODES // 2, (half + 1) * NODES // 2)
+            nc.tensor.matmul_mx(
+                out=acc_halves[half][:],
+                lhsT=w2_codes[:, a, local, :].bitcast(FP8X4),
+                lhsT_scale=w2_scales[:, a, local, :],
+                rhs=agg_codes[:, g, n_cols].bitcast(FP8X4),
+                rhs_scale=agg_scales[:, g, n_cols],
+                start=(g == 0),
+                stop=(g == PASSES - 1),
+            )
+            if g == PASSES - 1:
+                if half == 1:
+                    add_bias(OUT_TILES - 2)
+                take_peak(half_peaks[:, half, :], acc_halves[half])
+
+        def finish_last_tiles():
+            o_tile = OUT_TILES - 1
+            bias_column = bias[:, o_tile : o_tile + 1]
+            nc.vector.tensor_scalar(
+                out=half_biased[:], in0=half_peaks[:, 0, :], scalar1=bias_column, scalar2=None, op0=ALU.add
+            )
+            nc.vector.scalar_tensor_tensor(
+                out=biased[:, o_tile, :],
+                in0=half_peaks[:, 1, :],
+                scalar=bias_column,
+                in1=half_biased[:],
+                op0=ALU.add,
+                op1=ALU.max,
+            )
+            store(OUT_TILES - 2, 2)
+
+        def take_peak(out, acc):
             nc.vector.tensor_reduce(
-                out=peaks[:, o_tile, :],
-                in_=acc_of[o_tile][:].rearrange("p (n q) -> p q n", q=PIXELS),
+                out=out,
+                in_=acc[:].rearrange("p (n q) -> p q n", q=PIXELS),
                 axis=mybir.AxisListType.X,
                 op=ALU.max,
             )
 
-        def finish(first_tile, n_tiles):
+        def add_bias(o_tile):
+            nc.vector.tensor_scalar(
+                out=biased[:, o_tile, :],
+                in0=peaks[:, o_tile, :],
+                scalar1=bias[:, o_tile : o_tile + 1],
+                scalar2=None,
+                op0=ALU.add,
+            )
+
+        def store(first_tile, n_tiles):
             done = slice(first_tile, first_tile + n_tiles)
-            for o_tile in range(first_tile, first_tile + n_tiles):
-                nc.vector.tensor_scalar(
-                    out=biased[:, o_tile, :],
-                    in0=peaks[:, o_tile, :],
-                    scalar1=bias[:, o_tile : o_tile + 1],
-                    scalar2=None,
-                    op0=ALU.add,
-                )
             nc.vector.scalar_tensor_tensor(
                 out=result[:, done, :],
                 in0=biased[:, done, :],
@@ -284,27 +330,28 @@ def tile_similargcn_pb_k_kernel(tc, weight, hid, W2, b2, out):
                 out=weight_raw[:, 2 * pair : 2 * pair + 2, :],
                 in_=weight[2 * pair * P : (2 * pair + 2) * P, :].rearrange("(a p) j -> p a j", p=P),
             )
+        load_w2_tiles(0, 0, 1)
+        load_w2_tiles(0, 1, 1)
         load_hid(1)
-        load_w2(0, 2)
+        load_w2_tiles(0, 2, 2)
         nc.sync.dma_start(out=bias_rows[0:OUT_TILES, :], in_=b2.rearrange("(a p) -> a p", p=P))
         load_hid(2)
         load_w2(1, 1)
         load_hid(3)
         load_hid(4)
         load_w2(2, 1)
-        load_w2(3, 1)
         weight_grouped = const.tile([P, NODES, 2], F32, align_bytes=64)
         weight_codes = const.tile([P, NODES], U32, align_bytes=64)
         weight_scales = const.tile([P, NODES], U8, align_bytes=64)
 
         def flip_weight(pair):
             pair_words = weight_raw[:, 2 * pair : 2 * pair + 2, :].bitcast(F32)
-            flip_two_row_tiles(
+            flip_pair(
                 nc,
                 banks,
                 identity,
                 lambda a, u, words=pair_words: words[:, a, u : WORDS : 2],
-                weight_grouped[:, 2 * pair * P : (2 * pair + 2) * P, :],
+                weight_grouped[:, 2 * pair * P : (2 * pair + 2) * P, :].rearrange("p (a r) u -> p a r u", a=2),
             )
 
         def quantise_weight(pair):
@@ -337,8 +384,12 @@ def tile_similargcn_pb_k_kernel(tc, weight, hid, W2, b2, out):
         quantise_weight(0)
         quantise_weight(1)
         regroup_hid(1)
+        start_flips(0)
+        flip_tile(0, 0, 0)
+        flip_tile(0, 1, 0)
         aggregate_pass(0)
-        flip_w2(0)
+        flip_tile(0, 2, 0)
+        flip_tile(0, 3, 0)
         quantise_hid(1)
         quantise_agg(0)
         aggregate_pass(1)
@@ -368,16 +419,26 @@ def tile_similargcn_pb_k_kernel(tc, weight, hid, W2, b2, out):
                 quantise_hid(s + 3)
             if s >= (ROUNDS + 1) and s + 2 < len(steps):
                 split_w2(s + 2)
-            for i in range(STEP_PAIRS):
-                if s < ROUNDS:
-                    g = s * ROUND_PASSES + i // NODE_TILES
-                    aggregate(g, i % NODE_TILES)
-                    if i % NODE_TILES == NODE_TILES - 1 and i < STEP_PAIRS - 1:
-                        quantise_agg(g)
-                multiply(s - 1, i)
+            n_mult = steps[s - 1][1] * steps[s - 1][3]
+            n_agg = ROUND_PASSES * NODE_TILES if s < ROUNDS else 0
+            done = 0
+            for i in range(n_agg):
+                g = s * ROUND_PASSES + i // NODE_TILES
+                aggregate(g, i % NODE_TILES)
+                if i % NODE_TILES == NODE_TILES - 1 and i < n_agg - 1:
+                    quantise_agg(g)
+                while done * n_agg < n_mult * (i + 1):
+                    multiply(s - 1, done)
+                    done = done + 1
+            while done < n_mult:
+                multiply(s - 1, done)
+                done = done + 1
             if s < (ROUNDS + 1) and s + 2 < len(steps):
                 split_w2(s + 2)
             if s + 1 < len(steps):
                 flip_w2(s + 1)
             if s == ROUNDS + 1:
-                finish(0, NODE_TILES)
+                for o_tile in range(4):
+                    add_bias(o_tile)
+                store(0, 4)
+        finish_last_tiles()

@@ -64,9 +64,10 @@ def tile_similargcn_pb_k_kernel(tc, weight, hid, W2, b2, out):
             for first_pass in range(0, PASSES, step_passes):
                 steps.append((first_tile, n_tiles, first_pass, step_passes))
 
-        hid_units = [(g, 1) for g in range(FIRST_SINGLES)] + [
+        hid_loads = [(g, 1) for g in range(FIRST_SINGLES)] + [
             (g, ROUND_PASSES) for g in range(FIRST_SINGLES, PASSES, ROUND_PASSES)
         ]
+        hid_units = [(g, 1) for g in range(PASSES)]
         unit_of_pass = {}
         for c, (first_pass, n_passes) in enumerate(hid_units):
             for local in range(n_passes):
@@ -82,8 +83,8 @@ def tile_similargcn_pb_k_kernel(tc, weight, hid, W2, b2, out):
         acc_of = {}
         acc_halves = []
 
-        agg_codes = keep.tile([P, PASSES, NODES], U32, align_bytes=64)
-        agg_scales = keep.tile([P, PASSES, NODES], U8, align_bytes=64)
+        agg_codes = keep.tile([P, PASSES, NODES], U32, align_bytes=256)
+        agg_scales = keep.tile([P, PASSES, NODES], U8, align_bytes=256)
         peaks = keep.tile([P, OUT_TILES, PIXELS], F32)
         biased = keep.tile([P, OUT_TILES, PIXELS], F32)
         result = keep.tile([P, OUT_TILES, PIXELS], F32)
@@ -92,7 +93,7 @@ def tile_similargcn_pb_k_kernel(tc, weight, hid, W2, b2, out):
         out_rows = out.rearrange("x (a p) h w -> p (x a) (h w)", p=P)
 
         def load_hid(c):
-            first_pass, n_passes = hid_units[c]
+            first_pass, n_passes = hid_loads[c]
             hid_raw = raw.tile([P, PACK, n_passes * K_PASS], BF16, tag="hid_raw")
             nc.sync.dma_start(
                 out=hid_raw[:],
@@ -100,7 +101,8 @@ def tile_similargcn_pb_k_kernel(tc, weight, hid, W2, b2, out):
                     "(q t) f -> q t f", t=PACK
                 ),
             )
-            hid_raw_of[c] = hid_raw
+            for local in range(n_passes):
+                hid_raw_of[first_pass + local] = hid_raw[:, :, local * K_PASS : (local + 1) * K_PASS]
 
         def load_w2(s, n_loads=1):
             n_tiles = steps[s][1]
@@ -125,7 +127,7 @@ def tile_similargcn_pb_k_kernel(tc, weight, hid, W2, b2, out):
             first_tile, n_tiles, first_pass, step_passes = steps[s]
             n_split = split_tiles(s)
             if n_split > 0:
-                w2_split = stage.tile([P, n_split, step_passes, 2, P], F32, tag="w2_split", align_bytes=64)
+                w2_split = stage.tile([P, n_split, step_passes, 2, P], F32, tag="w2_split", align_bytes=256)
                 nc.vector.tensor_copy(
                     out=w2_split[:].rearrange("p a l u q -> p (a l) u q"),
                     in_=w2_raw_of[s][:, 0:n_split, :].bitcast(F32).rearrange("p a (l q u) -> p (a l) u q", q=P, u=2),
@@ -134,7 +136,7 @@ def tile_similargcn_pb_k_kernel(tc, weight, hid, W2, b2, out):
 
         def start_flips(s):
             first_tile, n_tiles, first_pass, step_passes = steps[s]
-            w2_grouped = stage.tile([P, n_tiles, step_passes, P, 2], F32, tag="w2_grouped", align_bytes=64)
+            w2_grouped = stage.tile([P, n_tiles, step_passes, P, 2], F32, tag="w2_grouped", align_bytes=256)
             w2_grouped_of[s] = w2_grouped
 
         def flip_tile(s, a, first_local):
@@ -158,8 +160,8 @@ def tile_similargcn_pb_k_kernel(tc, weight, hid, W2, b2, out):
 
         def quantise_w2(s):
             first_tile, n_tiles, first_pass, step_passes = steps[s]
-            w2_codes = codes.tile([P, n_tiles, step_passes, P], U32, tag="w2_codes", align_bytes=64)
-            w2_scales = codes.tile([P, n_tiles, step_passes, P], U8, tag="w2_scales", align_bytes=64)
+            w2_codes = codes.tile([P, n_tiles, step_passes, P], U32, tag="w2_codes", align_bytes=256)
+            w2_scales = codes.tile([P, n_tiles, step_passes, P], U8, tag="w2_scales", align_bytes=256)
             calls = (n_tiles,) if s < ROUNDS else (1, 1)
             first = 0
             for count in calls:
@@ -174,17 +176,17 @@ def tile_similargcn_pb_k_kernel(tc, weight, hid, W2, b2, out):
 
         def regroup_hid(c):
             width = hid_units[c][1] * K_PASS
-            hid_grouped = stage.tile([P, width, PACK], BF16, tag="hid_grouped", align_bytes=64)
+            hid_grouped = stage.tile([P, width, PACK], BF16, tag="hid_grouped", bufs=4, align_bytes=256)
             nc.vector.tensor_copy(
                 out=hid_grouped[:].rearrange("p (i c) t -> p c t i", i=PACK),
-                in_=hid_raw_of[c][:].rearrange("p t (c i) -> p c t i", i=PACK),
+                in_=hid_raw_of[c].rearrange("p t (c i) -> p c t i", i=PACK),
             )
             hid_grouped_of[c] = hid_grouped
 
         def quantise_hid(c):
             width = hid_units[c][1] * K_PASS
-            hid_codes = stage.tile([P, width], U32, tag="hid_codes", bufs=3, align_bytes=64)
-            hid_scales = stage.tile([P, width], U8, tag="hid_scales", bufs=3, align_bytes=64)
+            hid_codes = stage.tile([P, width], U32, tag="hid_codes", bufs=6, align_bytes=256)
+            hid_scales = stage.tile([P, width], U8, tag="hid_scales", bufs=6, align_bytes=256)
             nc.vector.quantize_mx(
                 out=hid_codes[:].bitcast(FP8X4),
                 scales=hid_scales[:],
@@ -196,7 +198,7 @@ def tile_similargcn_pb_k_kernel(tc, weight, hid, W2, b2, out):
 
         def aggregate(g, mt):
             if mt == 0:
-                agg_grouped = stage.tile([P, NODES, PACK], BF16, bufs=3, align_bytes=64)
+                agg_grouped = stage.tile([P, NODES, PACK], BF16, bufs=3, align_bytes=256)
                 agg_grouped_of[g] = agg_grouped
             c, local = unit_of_pass[g]
             hid_codes, hid_scales = hid_codes_of[c]
@@ -340,9 +342,9 @@ def tile_similargcn_pb_k_kernel(tc, weight, hid, W2, b2, out):
         load_hid(3)
         load_hid(4)
         load_w2(2, 1)
-        weight_grouped = const.tile([P, NODES, 2], F32, align_bytes=64)
-        weight_codes = const.tile([P, NODES], U32, align_bytes=64)
-        weight_scales = const.tile([P, NODES], U8, align_bytes=64)
+        weight_grouped = const.tile([P, NODES, 2], F32, align_bytes=256)
+        weight_codes = const.tile([P, NODES], U32, align_bytes=256)
+        weight_scales = const.tile([P, NODES], U8, align_bytes=256)
 
         def flip_weight(pair):
             pair_words = weight_raw[:, 2 * pair : 2 * pair + 2, :].bitcast(F32)
@@ -412,11 +414,12 @@ def tile_similargcn_pb_k_kernel(tc, weight, hid, W2, b2, out):
             if s > 1 and s <= ROUNDS:
                 quantise_agg(s * ROUND_PASSES - 1)
             if s + 1 < ROUNDS:
-                regroup_hid(s + 3)
+                regroup_hid(2 * s + 2)
             if s < len(steps):
                 quantise_w2(s)
             if s + 1 < ROUNDS:
-                quantise_hid(s + 3)
+                quantise_hid(2 * s + 2)
+                regroup_hid(2 * s + 3)
             if s >= (ROUNDS + 1) and s + 2 < len(steps):
                 split_w2(s + 2)
             n_mult = steps[s - 1][1] * steps[s - 1][3]
@@ -427,6 +430,8 @@ def tile_similargcn_pb_k_kernel(tc, weight, hid, W2, b2, out):
                 aggregate(g, i % NODE_TILES)
                 if i % NODE_TILES == NODE_TILES - 1 and i < n_agg - 1:
                     quantise_agg(g)
+                    if s + 1 < ROUNDS:
+                        quantise_hid(2 * s + 3)
                 while done * n_agg < n_mult * (i + 1):
                     multiply(s - 1, done)
                     done = done + 1

@@ -33,7 +33,7 @@ FLOPS = 2 * NODES * NODES * HIDDEN + 2 * NODES * HIDDEN * OUT
 
 
 def split_tiles(s):
-    return 2 if s >= ROUNDS else (1 if s > 4 else 0)
+    return 2 if s >= ROUNDS else (1 if s > 3 else 0)
 
 
 def flip_pair(nc, banks, identity, word_slice, grouped_words):
@@ -129,8 +129,8 @@ def tile_similargcn_pb_k_kernel(tc, weight, hid, W2, b2, out):
             if n_split > 0:
                 w2_split = stage.tile([P, n_split, step_passes, 2, P], F32, tag="w2_split", align_bytes=256)
                 nc.vector.tensor_copy(
-                    out=w2_split[:].rearrange("p a l u q -> p (a l) u q"),
-                    in_=w2_raw_of[s][:, 0:n_split, :].bitcast(F32).rearrange("p a (l q u) -> p (a l) u q", q=P, u=2),
+                    out=w2_split[:].rearrange("p a l u q -> p (a l) q u"),
+                    in_=w2_raw_of[s][:, 0:n_split, :].bitcast(F32).rearrange("p a (l q u) -> p (a l) q u", q=P, u=2),
                 )
                 w2_split_of[s] = w2_split
 

@@ -17,6 +17,7 @@ NODES = 512
 HIDDEN = 8192
 OUT = 768
 PIXELS = 64
+SAMPLES = 8
 SLOPE = 0.01
 
 NODE_TILES = NODES // P
@@ -26,7 +27,7 @@ ROUND_PASSES = 2
 ROUNDS = PASSES // ROUND_PASSES
 GROUPS = ((0, 4, 2), (4, 2, 4))
 HID_AHEAD = 2
-FIRST_SINGLES = 4
+FIRST_SINGLES = 2
 W2_AHEAD = 2
 
 FLOPS = 2 * NODES * NODES * HIDDEN + 2 * NODES * HIDDEN * OUT
@@ -88,8 +89,6 @@ def tile_similargcn_pb_k_kernel(tc, weight, hid, W2, b2, out):
         peaks = keep.tile([P, OUT_TILES, PIXELS], F32)
         biased = keep.tile([P, OUT_TILES, PIXELS], F32)
         result = keep.tile([P, OUT_TILES, PIXELS], F32)
-        half_peaks = keep.tile([P, 2, PIXELS], F32)
-        half_biased = keep.tile([P, PIXELS], F32)
         out_rows = out.rearrange("x (a p) h w -> p (x a) (h w)", p=P)
 
         def load_hid(c):
@@ -256,7 +255,7 @@ def tile_similargcn_pb_k_kernel(tc, weight, hid, W2, b2, out):
                 stop=(g == PASSES - 1),
             )
             if g == PASSES - 1:
-                take_peak(peaks[:, first_tile + a, :], acc_of[first_tile + a])
+                take_peak(first_tile + a, acc_of[first_tile + a], 0, NODE_TILES)
 
         def multiply_half(s, a, local, half):
             g = steps[s][2] + local
@@ -272,30 +271,33 @@ def tile_similargcn_pb_k_kernel(tc, weight, hid, W2, b2, out):
                 stop=(g == PASSES - 1),
             )
             if g == PASSES - 1:
+                n_half = NODE_TILES // 2
                 if half == 1:
                     add_bias(OUT_TILES - 2)
-                take_peak(half_peaks[:, half, :], acc_halves[half])
+                take_peak(OUT_TILES - 1, acc_halves[half], half * n_half, n_half)
+                if half == 1:
+                    add_bias_half(0)
+                    leak(OUT_TILES - 2)
+                    add_bias_half(1)
 
-        def finish_last_tiles():
+        def pixels(tile, o_tile):
+            return tile[:, o_tile, :].rearrange("p (i a) -> p i a", a=NODE_TILES)
+
+        def add_bias_half(half):
             o_tile = OUT_TILES - 1
-            bias_column = bias[:, o_tile : o_tile + 1]
+            tiles = slice(half * NODE_TILES // 2, (half + 1) * NODE_TILES // 2)
             nc.vector.tensor_scalar(
-                out=half_biased[:], in0=half_peaks[:, 0, :], scalar1=bias_column, scalar2=None, op0=ALU.add
-            )
-            nc.vector.scalar_tensor_tensor(
-                out=biased[:, o_tile, :],
-                in0=half_peaks[:, 1, :],
-                scalar=bias_column,
-                in1=half_biased[:],
+                out=pixels(biased, o_tile)[:, :, tiles],
+                in0=pixels(peaks, o_tile)[:, :, tiles],
+                scalar1=bias[:, o_tile : o_tile + 1],
+                scalar2=None,
                 op0=ALU.add,
-                op1=ALU.max,
             )
-            store(OUT_TILES - 2, 2)
 
-        def take_peak(out, acc):
+        def take_peak(o_tile, acc, first_tile, n_tiles):
             nc.vector.tensor_reduce(
-                out=out,
-                in_=acc[:].rearrange("p (n q) -> p q n", q=PIXELS),
+                out=pixels(peaks, o_tile)[:, :, first_tile : first_tile + n_tiles],
+                in_=acc[:].rearrange("p (a n i) -> p i a n", a=n_tiles, n=SAMPLES),
                 axis=mybir.AxisListType.X,
                 op=ALU.max,
             )
@@ -309,7 +311,7 @@ def tile_similargcn_pb_k_kernel(tc, weight, hid, W2, b2, out):
                 op0=ALU.add,
             )
 
-        def store(first_tile, n_tiles):
+        def leak(first_tile, n_tiles=1):
             done = slice(first_tile, first_tile + n_tiles)
             nc.vector.scalar_tensor_tensor(
                 out=result[:, done, :],
@@ -319,6 +321,9 @@ def tile_similargcn_pb_k_kernel(tc, weight, hid, W2, b2, out):
                 op0=ALU.mult,
                 op1=ALU.max,
             )
+
+        def send(first_tile, n_tiles):
+            done = slice(first_tile, first_tile + n_tiles)
             nc.sync.dma_start(out=out_rows[:, done, :], in_=result[:, done, :])
 
         identity = const.tile([P, P], F32)
@@ -330,7 +335,7 @@ def tile_similargcn_pb_k_kernel(tc, weight, hid, W2, b2, out):
         for pair in range(NODE_TILES // 2):
             nc.sync.dma_start(
                 out=weight_raw[:, 2 * pair : 2 * pair + 2, :],
-                in_=weight[2 * pair * P : (2 * pair + 2) * P, :].rearrange("(a p) j -> p a j", p=P),
+                in_=weight.rearrange("(p a) j -> p a j", a=NODE_TILES)[:, 2 * pair : 2 * pair + 2, :],
             )
         load_w2_tiles(0, 0, 1)
         load_w2_tiles(0, 1, 1)
@@ -338,9 +343,8 @@ def tile_similargcn_pb_k_kernel(tc, weight, hid, W2, b2, out):
         load_w2_tiles(0, 2, 2)
         nc.sync.dma_start(out=bias_rows[0:OUT_TILES, :], in_=b2.rearrange("(a p) -> a p", p=P))
         load_hid(2)
-        load_w2(1, 1)
+        load_w2(1, 2)
         load_hid(3)
-        load_hid(4)
         load_w2(2, 1)
         weight_grouped = const.tile([P, NODES, 2], F32, align_bytes=256)
         weight_codes = const.tile([P, NODES], U32, align_bytes=256)
@@ -408,7 +412,7 @@ def tile_similargcn_pb_k_kernel(tc, weight, hid, W2, b2, out):
 
         for s in range(1, len(steps) + 1):
             if s + HID_AHEAD < ROUNDS:
-                load_hid(s + HID_AHEAD + 3 - 1)
+                load_hid(s + HID_AHEAD + 1)
             if s + W2_AHEAD < len(steps):
                 load_w2(s + W2_AHEAD, 1)
             if s > 1 and s <= ROUNDS:
@@ -445,5 +449,7 @@ def tile_similargcn_pb_k_kernel(tc, weight, hid, W2, b2, out):
             if s == ROUNDS + 1:
                 for o_tile in range(4):
                     add_bias(o_tile)
-                store(0, 4)
-        finish_last_tiles()
+                leak(0, 4)
+                send(0, 4)
+        leak(OUT_TILES - 1)
+        send(OUT_TILES - 2, 2)

@@ -177,8 +177,8 @@ def tile_similargcn_pb_k_kernel(tc, weight, hid, W2, b2, out):
             width = hid_units[c][1] * K_PASS
             hid_grouped = stage.tile([P, width, PACK], BF16, tag="hid_grouped", bufs=4, align_bytes=256)
             nc.vector.tensor_copy(
-                out=hid_grouped[:].rearrange("p (i c) t -> p c t i", i=PACK),
-                in_=hid_raw_of[c].rearrange("p t (c i) -> p c t i", i=PACK),
+                out=hid_grouped[:].rearrange("p (i b k) t -> p b i t k", i=PACK, k=2),
+                in_=hid_raw_of[c].rearrange("p t (b k i) -> p b i t k", i=PACK, k=2),
             )
             hid_grouped_of[c] = hid_grouped
 

import concourse.mybir as mybir
from concourse.masks import make_identity

F32 = mybir.dt.float32
BF16 = mybir.dt.bfloat16
U32 = mybir.dt.uint32
U8 = mybir.dt.uint8
FP8X4 = mybir.dt.float8_e4m3fn_x4
ALU = mybir.AluOpType

P = 128
PACK = 4
K_PASS = P * PACK
WORDS = K_PASS // 2

NODES = 512
HIDDEN = 8192
OUT = 768
PIXELS = 64
SAMPLES = 8
SLOPE = 0.01

NODE_TILES = NODES // P
OUT_TILES = OUT // P
PASSES = HIDDEN // K_PASS
ROUND_PASSES = 2
ROUNDS = PASSES // ROUND_PASSES
GROUPS = ((0, 4, 2), (4, 2, 4))
HID_AHEAD = 2
FIRST_SINGLES = 2
W2_AHEAD = 2

FLOPS = 2 * NODES * NODES * HIDDEN + 2 * NODES * HIDDEN * OUT


def split_tiles(s):
    return 2 if s >= ROUNDS else (1 if s > 3 else 0)


def flip_pair(nc, banks, identity, word_slice, grouped_words):
    bank = banks.tile([P, PACK, P], F32, tag="bank")
    for a in range(2):
        for u in range(2):
            nc.tensor.transpose(bank[:, 2 * a + u, :], word_slice(a, u), identity[:])
    nc.scalar.copy(
        out=grouped_words,
        in_=bank[:].rearrange("p (a u) r -> p a r u", a=2),
    )


def tile_similargcn_pb_k_kernel(tc, weight, hid, W2, b2, out):
    nc = tc.nc
    with (
        tc.tile_pool(name="const", bufs=1) as const,
        tc.tile_pool(name="keep", bufs=1) as keep,
        tc.tile_pool(name="raw", bufs=4) as raw,
        tc.tile_pool(name="stage", bufs=2) as stage,
        tc.tile_pool(name="codes", bufs=3) as codes,
        tc.psum_pool(name="sums", bufs=1) as sums,
        tc.psum_pool(name="banks", bufs=4) as banks,
        tc.manual_schedule(),
    ):
        steps = []
        for first_tile, n_tiles, step_passes in GROUPS:
            for first_pass in range(0, PASSES, step_passes):
                steps.append((first_tile, n_tiles, first_pass, step_passes))

        hid_loads = [(g, 1) for g in range(FIRST_SINGLES)] + [
            (g, ROUND_PASSES) for g in range(FIRST_SINGLES, PASSES, ROUND_PASSES)
        ]
        hid_units = [(g, 1) for g in range(PASSES)]
        unit_of_pass = {}
        for c, (first_pass, n_passes) in enumerate(hid_units):
            for local in range(n_passes):
                unit_of_pass[first_pass + local] = (c, local)

        hid_raw_of = {}
        hid_grouped_of = {}
        hid_codes_of = {}
        w2_raw_of = {}
        w2_split_of = {}
        w2_grouped_of = {}
        w2_codes_of = {}
        acc_of = {}
        acc_halves = []

        agg_codes = keep.tile([P, PASSES, NODES], U32, align_bytes=256)
        agg_scales = keep.tile([P, PASSES, NODES], U8, align_bytes=256)
        peaks = keep.tile([P, OUT_TILES, PIXELS], F32)
        biased = keep.tile([P, OUT_TILES, PIXELS], F32)
        result = keep.tile([P, OUT_TILES, PIXELS], F32)
        out_rows = out.rearrange("x (a p) h w -> p (x a) (h w)", p=P)

        def load_hid(c):
            first_pass, n_passes = hid_loads[c]
            hid_raw = raw.tile([P, PACK, n_passes * K_PASS], BF16, tag="hid_raw")
            nc.sync.dma_start(
                out=hid_raw[:],
                in_=hid[:, first_pass * K_PASS : (first_pass + n_passes) * K_PASS].rearrange(
                    "(q t) f -> q t f", t=PACK
                ),
            )
            for local in range(n_passes):
                hid_raw_of[first_pass + local] = hid_raw[:, :, local * K_PASS : (local + 1) * K_PASS]

        def load_w2(s, n_loads=1):
            n_tiles = steps[s][1]
            per_load = n_tiles // n_loads
            for first in range(0, n_tiles, per_load):
                load_w2_tiles(s, first, per_load)

        def load_w2_tiles(s, first, per_load):
            first_tile, n_tiles, first_pass, step_passes = steps[s]
            if s not in w2_raw_of:
                w2_raw = raw.tile([P, n_tiles, step_passes * K_PASS], BF16, tag="w2_raw", bufs=5)
                w2_raw_of[s] = w2_raw
            nc.sync.dma_start(
                out=w2_raw_of[s][:, first : first + per_load, :],
                in_=W2[
                    (first_tile + first) * P : (first_tile + first + per_load) * P,
                    first_pass * K_PASS : (first_pass + step_passes) * K_PASS,
                ].rearrange("(a p) f -> p a f", p=P),
            )

        def split_w2(s):
            first_tile, n_tiles, first_pass, step_passes = steps[s]
            n_split = split_tiles(s)
            if n_split > 0:
                w2_split = stage.tile([P, n_split, step_passes, 2, P], F32, tag="w2_split", align_bytes=256)
                nc.vector.tensor_copy(
                    out=w2_split[:].rearrange("p a l u q -> p (a l) q u"),
                    in_=w2_raw_of[s][:, 0:n_split, :].bitcast(F32).rearrange("p a (l q u) -> p (a l) q u", q=P, u=2),
                )
                w2_split_of[s] = w2_split

        def start_flips(s):
            first_tile, n_tiles, first_pass, step_passes = steps[s]
            w2_grouped = stage.tile([P, n_tiles, step_passes, P, 2], F32, tag="w2_grouped", align_bytes=256)
            w2_grouped_of[s] = w2_grouped

        def flip_tile(s, a, first_local):
            raw_words = w2_raw_of[s][:].bitcast(F32)

            def word_slice(j, u):
                local = first_local + j
                if a < split_tiles(s):
                    return w2_split_of[s][:, a, local, u, :]
                first = local * WORDS + u
                return raw_words[:, a, first : first + WORDS - u : 2]

            flip_pair(nc, banks, identity, word_slice, w2_grouped_of[s][:, a, first_local : first_local + 2, :, :])

        def flip_w2(s):
            first_tile, n_tiles, first_pass, step_passes = steps[s]
            start_flips(s)
            for a in range(n_tiles):
                for first_local in range(0, step_passes, 2):
                    flip_tile(s, a, first_local)

        def quantise_w2(s):
            first_tile, n_tiles, first_pass, step_passes = steps[s]
            w2_codes = codes.tile([P, n_tiles, step_passes, P], U32, tag="w2_codes", align_bytes=256)
            w2_scales = codes.tile([P, n_tiles, step_passes, P], U8, tag="w2_scales", align_bytes=256)
            calls = (n_tiles,) if s < ROUNDS else (1, 1)
            first = 0
            for count in calls:
                part = slice(first, first + count)
                first = first + count
                nc.vector.quantize_mx(
                    out=w2_codes[:, part].rearrange("p a l o -> p (a l o)").bitcast(FP8X4),
                    scales=w2_scales[:, part].rearrange("p a l o -> p (a l o)"),
                    in_=w2_grouped_of[s][:, part].rearrange("p a l o u -> p (a l o u)").bitcast(BF16),
                )
            w2_codes_of[s] = (w2_codes, w2_scales)

        def regroup_hid(c):
            width = hid_units[c][1] * K_PASS
            hid_grouped = stage.tile([P, width, PACK], BF16, tag="hid_grouped", bufs=4, align_bytes=256)
            nc.vector.tensor_copy(
                out=hid_grouped[:].rearrange("p (i b k) t -> p b i t k", i=PACK, k=2),
                in_=hid_raw_of[c].rearrange("p t (b k i) -> p b i t k", i=PACK, k=2),
            )
            hid_grouped_of[c] = hid_grouped

        def quantise_hid(c):
            width = hid_units[c][1] * K_PASS
            hid_codes = stage.tile([P, width], U32, tag="hid_codes", bufs=6, align_bytes=256)
            hid_scales = stage.tile([P, width], U8, tag="hid_scales", bufs=6, align_bytes=256)
            nc.vector.quantize_mx(
                out=hid_codes[:].bitcast(FP8X4),
                scales=hid_scales[:],
                in_=hid_grouped_of[c][:].rearrange("p f t -> p (f t)"),
            )
            hid_codes_of[c] = (hid_codes, hid_scales)

        agg_grouped_of = {}

        def aggregate(g, mt):
            if mt == 0:
                agg_grouped = stage.tile([P, NODES, PACK], BF16, bufs=3, align_bytes=256)
                agg_grouped_of[g] = agg_grouped
            c, local = unit_of_pass[g]
            hid_codes, hid_scales = hid_codes_of[c]
            m_cols = slice(mt * P, (mt + 1) * P)
            bank = banks.tile([P, PACK, P], F32, tag="bank")
            for t in range(PACK):
                first = (t * hid_units[c][1] + local) * P
                f_cols = slice(first, first + P)
                nc.tensor.matmul_mx(
                    out=bank[:, t, :],
                    lhsT=hid_codes[:, f_cols].bitcast(FP8X4),
                    lhsT_scale=hid_scales[:, f_cols],
                    rhs=weight_codes[:, m_cols].bitcast(FP8X4),
                    rhs_scale=weight_scales[:, m_cols],
                    start=True,
                    stop=True,
                )
            nc.scalar.copy(out=agg_grouped_of[g][:, m_cols, :], in_=bank[:].rearrange("p t m -> p m t"))

        def quantise_agg(g):
            nc.vector.quantize_mx(
                out=agg_codes[:, g, :].bitcast(FP8X4),
                scales=agg_scales[:, g, :],
                in_=agg_grouped_of[g][:].rearrange("p m t -> p (m t)"),
            )

        def multiply(s, i):
            first_tile, n_tiles, first_pass, step_passes = steps[s]
            last_step = s == len(steps) - 1
            by_tile = s in (ROUNDS - 1, ROUNDS, len(steps) - 1)
            local = i % step_passes if by_tile else i // n_tiles
            a = i // step_passes if by_tile else i % n_tiles
            g = first_pass + local
            w2_codes, w2_scales = w2_codes_of[s]
            if first_tile + a == OUT_TILES - 1:
                if g == 0:
                    for half in range(2):
                        acc_half = sums.tile([P, NODES // 2], F32, name="acc_half%d" % half, tag="acc%d" % (a + half))
                        acc_halves.append(acc_half)
                for j in range(2):
                    unit = 2 * local + j
                    half = unit // step_passes if last_step else j
                    pass_of_unit = unit % step_passes if last_step else local
                    multiply_half(s, a, pass_of_unit, half)
                return
            if g == 0:
                acc_of[first_tile + a] = sums.tile([P, NODES], F32, name="acc%d" % a, tag="acc%d" % a)
            nc.tensor.matmul_mx(
                out=acc_of[first_tile + a][:],
                lhsT=w2_codes[:, a, local, :].bitcast(FP8X4),
                lhsT_scale=w2_scales[:, a, local, :],
                rhs=agg_codes[:, g, :].bitcast(FP8X4),
                rhs_scale=agg_scales[:, g, :],
                start=(g == 0),
                stop=(g == PASSES - 1),
            )
            if g == PASSES - 1:
                take_peak(first_tile + a, acc_of[first_tile + a], 0, NODE_TILES)

        def multiply_half(s, a, local, half):
            g = steps[s][2] + local
            w2_codes, w2_scales = w2_codes_of[s]
            n_cols = slice(half * NODES // 2, (half + 1) * NODES // 2)
            nc.tensor.matmul_mx(
                out=acc_halves[half][:],
                lhsT=w2_codes[:, a, local, :].bitcast(FP8X4),
                lhsT_scale=w2_scales[:, a, local, :],
                rhs=agg_codes[:, g, n_cols].bitcast(FP8X4),
                rhs_scale=agg_scales[:, g, n_cols],
                start=(g == 0),
                stop=(g == PASSES - 1),
            )
            if g == PASSES - 1:
                n_half = NODE_TILES // 2
                if half == 1:
                    add_bias(OUT_TILES - 2)
                take_peak(OUT_TILES - 1, acc_halves[half], half * n_half, n_half)
                if half == 1:
                    add_bias_half(0)
                    leak(OUT_TILES - 2)
                    add_bias_half(1)

        def pixels(tile, o_tile):
            return tile[:, o_tile, :].rearrange("p (i a) -> p i a", a=NODE_TILES)

        def add_bias_half(half):
            o_tile = OUT_TILES - 1
            tiles = slice(half * NODE_TILES // 2, (half + 1) * NODE_TILES // 2)
            nc.vector.tensor_scalar(
                out=pixels(biased, o_tile)[:, :, tiles],
                in0=pixels(peaks, o_tile)[:, :, tiles],
                scalar1=bias[:, o_tile : o_tile + 1],
                scalar2=None,
                op0=ALU.add,
            )

        def take_peak(o_tile, acc, first_tile, n_tiles):
            nc.vector.tensor_reduce(
                out=pixels(peaks, o_tile)[:, :, first_tile : first_tile + n_tiles],
                in_=acc[:].rearrange("p (a n i) -> p i a n", a=n_tiles, n=SAMPLES),
                axis=mybir.AxisListType.X,
                op=ALU.max,
            )

        def add_bias(o_tile):
            nc.vector.tensor_scalar(
                out=biased[:, o_tile, :],
                in0=peaks[:, o_tile, :],
                scalar1=bias[:, o_tile : o_tile + 1],
                scalar2=None,
                op0=ALU.add,
            )

        def leak(first_tile, n_tiles=1):
            done = slice(first_tile, first_tile + n_tiles)
            nc.vector.scalar_tensor_tensor(
                out=result[:, done, :],
                in0=biased[:, done, :],
                scalar=SLOPE,
                in1=biased[:, done, :],
                op0=ALU.mult,
                op1=ALU.max,
            )

        def send(first_tile, n_tiles):
            done = slice(first_tile, first_tile + n_tiles)
            nc.sync.dma_start(out=out_rows[:, done, :], in_=result[:, done, :])

        identity = const.tile([P, P], F32)
        make_identity(nc, identity[:])
        bias_rows = const.tile([P, P], BF16)
        nc.vector.memset(bias_rows[:], 0.0)
        load_hid(0)
        weight_raw = const.tile([P, NODE_TILES, NODES], BF16)
        for pair in range(NODE_TILES // 2):
            nc.sync.dma_start(
                out=weight_raw[:, 2 * pair : 2 * pair + 2, :],
                in_=weight.rearrange("(p a) j -> p a j", a=NODE_TILES)[:, 2 * pair : 2 * pair + 2, :],
            )
        load_w2_tiles(0, 0, 1)
        load_w2_tiles(0, 1, 1)
        load_hid(1)
        load_w2_tiles(0, 2, 2)
        nc.sync.dma_start(out=bias_rows[0:OUT_TILES, :], in_=b2.rearrange("(a p) -> a p", p=P))
        load_hid(2)
        load_w2(1, 2)
        load_hid(3)
        load_w2(2, 1)
        weight_grouped = const.tile([P, NODES, 2], F32, align_bytes=256)
        weight_codes = const.tile([P, NODES], U32, align_bytes=256)
        weight_scales = const.tile([P, NODES], U8, align_bytes=256)

        def flip_weight(pair):
            pair_words = weight_raw[:, 2 * pair : 2 * pair + 2, :].bitcast(F32)
            flip_pair(
                nc,
                banks,
                identity,
                lambda a, u, words=pair_words: words[:, a, u : WORDS : 2],
                weight_grouped[:, 2 * pair * P : (2 * pair + 2) * P, :].rearrange("p (a r) u -> p a r u", a=2),
            )

        def quantise_weight(pair):
            m_cols = slice(2 * pair * P, (2 * pair + 2) * P)
            nc.vector.quantize_mx(
                out=weight_codes[:, m_cols].bitcast(FP8X4),
                scales=weight_scales[:, m_cols],
                in_=weight_grouped[:, m_cols, :].rearrange("p m u -> p (m u)").bitcast(BF16),
            )

        def aggregate_pass(g):
            for mt in range(NODE_TILES):
                aggregate(g, mt)

        bias_rows_f32 = const.tile([P, P], F32)
        bias = const.tile([P, OUT_TILES], F32)

        def spread_bias():
            nc.vector.tensor_copy(out=bias_rows_f32[:], in_=bias_rows[:])

        def flip_bias():
            bias_bank = banks.tile([P, PACK, P], F32, tag="bank")
            nc.tensor.transpose(bias_bank[:, 0, :], bias_rows_f32[:], identity[:])
            nc.scalar.copy(out=bias[:], in_=bias_bank[:, 0, 0:OUT_TILES])

        regroup_hid(0)
        flip_weight(0)
        flip_weight(1)
        quantise_hid(0)
        quantise_weight(0)
        quantise_weight(1)
        regroup_hid(1)
        start_flips(0)
        flip_tile(0, 0, 0)
        flip_tile(0, 1, 0)
        aggregate_pass(0)
        flip_tile(0, 2, 0)
        flip_tile(0, 3, 0)
        quantise_hid(1)
        quantise_agg(0)
        aggregate_pass(1)
        spread_bias()
        regroup_hid(2)
        quantise_w2(0)
        quantise_hid(2)
        regroup_hid(3)
        quantise_agg(1)
        quantise_hid(3)
        flip_w2(1)
        flip_bias()
        split_w2(2)

        for s in range(1, len(steps) + 1):
            if s + HID_AHEAD < ROUNDS:
                load_hid(s + HID_AHEAD + 1)
            if s + W2_AHEAD < len(steps):
                load_w2(s + W2_AHEAD, 1)
            if s > 1 and s <= ROUNDS:
                quantise_agg(s * ROUND_PASSES - 1)
            if s + 1 < ROUNDS:
                regroup_hid(2 * s + 2)
            if s < len(steps):
                quantise_w2(s)
            if s + 1 < ROUNDS:
                quantise_hid(2 * s + 2)
                regroup_hid(2 * s + 3)
            if s >= (ROUNDS + 1) and s + 2 < len(steps):
                split_w2(s + 2)
            n_mult = steps[s - 1][1] * steps[s - 1][3]
            n_agg = ROUND_PASSES * NODE_TILES if s < ROUNDS else 0
            done = 0
            for i in range(n_agg):
                g = s * ROUND_PASSES + i // NODE_TILES
                aggregate(g, i % NODE_TILES)
                if i % NODE_TILES == NODE_TILES - 1 and i < n_agg - 1:
                    quantise_agg(g)
                    if s + 1 < ROUNDS:
                        quantise_hid(2 * s + 3)
                while done * n_agg < n_mult * (i + 1):
                    multiply(s - 1, done)
                    done = done + 1
            while done < n_mult:
                multiply(s - 1, done)
                done = done + 1
            if s < (ROUNDS + 1) and s + 2 < len(steps):
                split_w2(s + 2)
            if s + 1 < len(steps):
                flip_w2(s + 1)
            if s == ROUNDS + 1:
                for o_tile in range(4):
                    add_bias(o_tile)
                leak(0, 4)
                send(0, 4)
        leak(OUT_TILES - 1)
        send(OUT_TILES - 2, 2)
